import numpy as np
import ml_dtypes


def mxq(x, axis, fmt="e4m3"):
    dtype, down = {"e4m3": (ml_dtypes.float8_e4m3fn, 7), "e5m2": (ml_dtypes.float8_e5m2, 14)}[fmt]
    v = np.moveaxis(np.asarray(x, np.float32).astype(ml_dtypes.bfloat16).astype(np.float64), axis, -1)
    blocks = v.reshape(v.shape[:-1] + (-1, 32))
    amax = np.abs(blocks).max(-1, keepdims=True)
    byte = np.maximum(np.where(amax > 0, np.frexp(amax)[1] - 1 + 127, 0) - down, 1)
    scale = np.exp2(byte - 127.0)
    codes = (blocks / scale).astype(np.float32).astype(dtype).astype(np.float64)
    return np.moveaxis((codes * scale).reshape(v.shape), -1, axis)


WIDE = False


def mx_kscale(k):
    if not WIDE:
        return np.ones(k)
    levels = np.array([18, -18])
    if k % 512:
        return np.exp2(np.random.permutation(np.resize(levels, k // 32))).repeat(32)
    a = np.empty((k // 512, 16))
    for p in range(k // 512):
        a[p, :8] = np.random.permutation(np.resize(levels, 8))
        for g in range(8):
            far = levels[np.abs(levels - a[p, g]) >= 10]
            a[p, g + 8] = far[np.random.randint(len(far))]
    return np.exp2(a.ravel()).repeat(32)


BF16 = ml_dtypes.bfloat16


def bf(x):
    return np.asarray(x, np.float32).astype(BF16)


def f64(x):
    return np.asarray(x).astype(np.float64)


B, I, H, C, S = 1024, 512, 1024, 511, 3
EPSILON = 1e-6
CC = 1 + C
K = I + H


def new_state(invariant_input, equivariant_input, invariant_hidden, equivariant_hidden, W_left, W_right, W_ii, b_ii):
    eq_comb = np.concatenate([f64(equivariant_input)[..., None], f64(equivariant_hidden)], axis=-1)
    inv_comb = np.concatenate([f64(invariant_input), f64(invariant_hidden)], axis=-1)
    norm = np.sum(eq_comb * eq_comb, axis=-2, keepdims=True) + EPSILON
    xn = eq_comb / norm
    left = xn @ f64(W_left)
    right = xn @ f64(W_right)
    proj = np.sum(left * right, axis=-2)
    lin = inv_comb @ f64(W_ii)
    return np.tanh(proj + lin + f64(b_ii))


def setup_inputs():
    s = mx_kscale(B)[:, None]
    u = mx_kscale(H)
    ii0 = bf(np.random.standard_normal((B, I)))
    ei = bf(np.random.standard_normal((B, S)) * 0.125)
    ih0 = bf(np.random.standard_normal((B, H)))
    eh = bf(np.random.standard_normal((B, S, C)) * 0.125)
    wl = bf(np.random.standard_normal((CC, H)) * 0.15 / np.sqrt(CC))
    wr = bf(np.random.standard_normal((CC, H)) * 0.15 / np.sqrt(CC))
    wi0 = bf(np.random.standard_normal((K, H)) * 0.6 / np.sqrt(K))
    bi = bf(np.random.standard_normal(H) * 0.3)
    g = bf(np.random.standard_normal((B, H)) * np.exp2(np.random.randint(-6, 1, (B, 1))) * 4.0 / s * u)
    y = new_state(ii0, ei, ih0, eh, wl, wr, wi0, bi)
    return {
        "invariant_input": bf(f64(ii0) * s),
        "equivariant_input": ei,
        "invariant_hidden": bf(f64(ih0) * s),
        "equivariant_hidden": eh,
        "W_left": wl,
        "W_right": wr,
        "W_ii": bf(f64(wi0) / u),
        "b_ii": bi,
        "y": np.asarray(y, np.float32),
        "grad_out": g,
    }


def reference(invariant_input, equivariant_input, invariant_hidden, equivariant_hidden, W_left, W_right, W_ii, b_ii, y, grad_out):
    yf = f64(y)
    dz = f64(grad_out) * (1.0 - yf * yf)
    wh = f64(W_ii)[I:]
    inv_comb = np.concatenate([f64(invariant_input), f64(invariant_hidden)], axis=-1)
    dx = mxq(dz, 1, "e5m2") @ mxq(wh, 1, "e4m3").T
    dw = mxq(inv_comb, 0, "e4m3").T @ mxq(dz, 0, "e5m2")
    return dx, dw

@@ -1,0 +1,303 @@
+from contextlib import ExitStack
+
+import concourse.mybir as mybir
+from concourse.masks import make_identity
+
+B, I, H = 1024, 512, 1024
+K = I + H
+FLOPS = 2 * B * H * H + 2 * B * K * H
+BYTES = B * K * 2 + H * H * 2 + B * H * 4 + B * H * 2 + B * H * 4 + K * H * 4
+
+F32 = mybir.dt.float32
+BF16 = mybir.dt.bfloat16
+U32 = mybir.dt.uint32
+U8 = mybir.dt.uint8
+E4 = mybir.dt.float8_e4m3fn_x4
+E5 = mybir.dt.float8_e5m2_x4
+ALU = mybir.AluOpType
+ACT = mybir.ActivationFunctionType
+
+P = 128
+PACK = 4
+PASS = P * PACK
+
+
+def tile_ryeelman_pa_v_kernel(
+    tc, invariant_input, equivariant_input, invariant_hidden, equivariant_hidden,
+    W_left, W_right, W_ii, b_ii, y, grad_out, out_0, out_1,
+):
+    nc = tc.nc
+    with ExitStack() as ctx:
+        keep = ctx.enter_context(tc.tile_pool(name="keep", bufs=1))
+        wide = ctx.enter_context(tc.tile_pool(name="wide", bufs=10))
+        stage = ctx.enter_context(tc.tile_pool(name="stage", bufs=4))
+        turn = ctx.enter_context(tc.psum_pool(name="turn", bufs=3))
+        sums = ctx.enter_context(tc.psum_pool(name="sums", bufs=5))
+        ctx.enter_context(tc.manual_schedule())
+
+        def rows4(t, g):
+            return t[g * PASS : (g + 1) * PASS, :].rearrange("(p j) w -> p (j w)", j=PACK)
+
+        def mx_tile(name, cols):
+            codes = keep.tile([P, cols], U32, name=name + "_codes", align_bytes=64)
+            scales = keep.tile([P, cols], U8, name=name + "_scales", align_bytes=64)
+            return codes, scales
+
+        ident = keep.tile([P, P], F32, name="ident")
+        make_identity(nc, ident[:])
+
+        y_sb = [wide.tile([P, 2 * H], F32, name="y%d" % n, tag="wide") for n in range(4)]
+        g_sb = [keep.tile([P, PACK * H], BF16, name="g%d" % g) for g in range(2)]
+        w_sb = [keep.tile([P, PACK * H], BF16, name="w%d" % a) for a in range(2)]
+        xi_sb = [keep.tile([P, PACK * I], BF16, name="xi%d" % g) for g in range(2)]
+        xh_sb = [keep.tile([P, PACK * H], BF16, name="xh%d" % g) for g in range(2)]
+        dz_sb = [keep.tile([P, PACK * H], BF16, name="dz%d" % g) for g in range(2)]
+
+        def load_y(n, lo, hi):
+            c0 = (n % 2) * 2 * H
+            nc.sync.dma_start(out=y_sb[n][:, lo * H : hi * H], in_=rows4(y, n // 2)[:, c0 + lo * H : c0 + hi * H])
+
+        def load_g(g, lo, hi):
+            nc.sync.dma_start(out=g_sb[g][:, lo * H : hi * H], in_=rows4(grad_out, g)[:, lo * H : hi * H])
+
+        def load_w(a):
+            nc.sync.dma_start(out=w_sb[a][:], in_=rows4(W_ii, 1 + a))
+
+        def load_xi(g):
+            nc.sync.dma_start(out=xi_sb[g][:], in_=rows4(invariant_input, g))
+
+        def load_xh(g):
+            nc.sync.dma_start(out=xh_sb[g][:], in_=rows4(invariant_hidden, g))
+
+        dzf = [mx_tile("dzf%d" % n, 2 * P) for n in range(8)]
+        wq = {(a, G): mx_tile("wq%d%d" % (a, G), PASS) for a in range(2) for G in range(2)}
+        dzt = {(g, G): mx_tile("dzt%d%d" % (g, G), PASS) for g in range(2) for G in range(2)}
+        xq = {(c, g): mx_tile("xq%d%d" % (c, g), PASS) for c in range(3) for g in range(2)}
+        held = {}
+
+        def y_unit(n):
+            return y_sb[n // 2][:, (n % 2) * H : (n % 2 + 1) * H]
+
+        def square(n):
+            nc.scalar.activation(out=y_unit(n), in_=y_unit(n), func=ACT.Square)
+
+        def neg_dz(n):
+            cols = slice((n % 4) * H, (n % 4 + 1) * H)
+            nc.vector.scalar_tensor_tensor(
+                out=dz_sb[n // 4][:, cols], in0=y_unit(n), scalar=1.0, in1=g_sb[n // 4][:, cols],
+                op0=ALU.subtract, op1=ALU.mult,
+            )
+
+        def turn_dz(n):
+            words = dz_sb[n // 4][:, (n % 4) * H : (n % 4 + 1) * H].bitcast(F32)
+            bank = turn.tile([P, 4, P], F32, name="bank", tag="bank")
+            for G in range(2):
+                for u in range(2):
+                    nc.tensor.transpose(bank[:, 2 * G + u, :], words[:, 256 * G + u : 256 * (G + 1) : 2], ident[:])
+            held["dzbank", n] = bank
+
+        def fetch_dz(n):
+            grouped = stage.tile([P, H], BF16, name="dzT", tag="dzT", align_bytes=64, bufs=3)
+            nc.scalar.copy(
+                out=grouped[:].bitcast(F32).rearrange("q (G r u) -> q G r u", G=2, u=2),
+                in_=held["dzbank", n][:].rearrange("q (G u) r -> q G r u", G=2),
+            )
+            held["dzT", n] = grouped
+
+        def quant(dst, src, fmt):
+            nc.vector.quantize_mx(out=dst[0][:].bitcast(fmt), scales=dst[1][:], in_=src[:])
+
+        def quant_dzf(n):
+            quant(dzf[n], held["dzT", n], E5)
+
+        def turn_w(a, G, tp):
+            words = w_sb[a][:].bitcast(F32)
+            bank = turn.tile([P, 4, P], F32, name="bank", tag="bank")
+            for t2 in range(2):
+                c0 = (2 * tp + t2) * 512 + 256 * G
+                for u in range(2):
+                    nc.tensor.transpose(bank[:, 2 * t2 + u, :], words[:, c0 + u : c0 + 256 : 2], ident[:])
+            held["wbank", a, G, tp] = bank
+
+        def fetch_w(a, G, tp):
+            if tp == 0:
+                held["wT", a, G] = stage.tile([P, PACK * PASS], BF16, name="wT", tag="grouped", align_bytes=64)
+            view = held["wT", a, G][:].bitcast(F32).rearrange("q (r s) -> q r s", s=8)
+            nc.scalar.copy(out=view[:, :, 4 * tp : 4 * tp + 4], in_=held["wbank", a, G, tp][:].rearrange("q s r -> q r s"))
+
+        def quant_w(a, G):
+            quant(wq[a, G], held["wT", a, G], E4)
+
+        def weave(key, src):
+            grouped = stage.tile([P, PACK * PASS], BF16, name="woven", tag="grouped", align_bytes=64)
+            nc.vector.tensor_copy(
+                out=grouped[:].rearrange("p (c i t) -> p c t i", i=4, t=PACK),
+                in_=src.rearrange("p t (c i) -> p c t i", i=4),
+            )
+            held[key] = grouped
+
+        def weave_dz(g, G):
+            weave(("dzw", g, G), dz_sb[g][:].rearrange("p (t h) -> p t h", t=PACK)[:, :, G * PASS : (G + 1) * PASS])
+
+        def quant_dzt(g, G):
+            quant(dzt[g, G], held["dzw", g, G], E5)
+
+        def weave_x(c, g):
+            if c == 0:
+                src = xi_sb[g][:].rearrange("p (t f) -> p t f", t=PACK)
+            else:
+                src = xh_sb[g][:].rearrange("p (t f) -> p t f", t=PACK)[:, :, (c - 1) * PASS : c * PASS]
+            weave(("xw", c, g), src)
+
+        def quant_x(c, g):
+            quant(xq[c, g], held["xw", c, g], E4)
+
+        def product(key, lhs, lhs_fmt, rhs, rhs_fmt):
+            acc = sums.tile([P, PASS], F32, name="acc", tag="acc")
+            for k in range(2):
+                (lc, ls), cols = lhs[k]
+                rc, rs = rhs[k]
+                nc.tensor.matmul_mx(
+                    out=acc[:], lhsT=lc[:, cols].bitcast(lhs_fmt), lhsT_scale=ls[:, cols],
+                    rhs=rc[:].bitcast(rhs_fmt), rhs_scale=rs[:], start=(k == 0), stop=(k == 1),
+                )
+            held[key] = acc
+
+        def mm0(n, a):
+            product(("acc0", n, a), [(dzf[n], slice(G * P, (G + 1) * P)) for G in range(2)], E5,
+                    [wq[a, G] for G in range(2)], E4)
+
+        def mm1(m, G):
+            cols = slice((m % 4) * P, (m % 4 + 1) * P)
+            product(("acc1", m, G), [(xq[m // 4, g], cols) for g in range(2)], E4, [dzt[g, G] for g in range(2)], E5)
+
+        def drain(name, n, half, on_vector):
+            if (name, n // 2) not in held:
+                held[name, n // 2] = wide.tile([P, 2 * H], F32, name=name, tag="wide")
+            c0 = (n % 2) * H + half * PASS
+            dst = held[name, n // 2][:, c0 : c0 + PASS]
+            acc = held["acc" + name[-1], n, half]
+            if on_vector:
+                nc.vector.tensor_scalar(out=dst, in0=acc[:], scalar1=-1.0, scalar2=None, op0=ALU.mult)
+            else:
+                nc.scalar.activation(out=dst, in_=acc[:], func=ACT.Copy, scale=-1.0)
+
+        def store0(pair):
+            c0 = (pair % 2) * 2 * H
+            nc.sync.dma_start(out=rows4(out_0, pair // 2)[:, c0 : c0 + 2 * H], in_=held["o0", pair][:])
+
+        def store1(m, count):
+            src = held["o1", m // 2][:, (m % 2) * H : (m % 2 + count) * H]
+            nc.sync.dma_start(
+                out=out_1[m * P : (m + count) * P, :].rearrange("(t p) h -> p t h", p=P),
+                in_=src.rearrange("p (t h) -> p t h", t=count),
+            )
+
+        load_y(0, 0, 1)
+        load_g(0, 0, 2)
+        load_y(0, 1, 2)
+        load_w(0)
+        load_y(1, 0, 2)
+        load_g(0, 2, 4)
+        load_w(1)
+        load_y(2, 0, 2)
+        load_g(1, 0, 4)
+        load_y(3, 0, 2)
+        load_xi(0)
+        load_xi(1)
+        load_xh(0)
+        load_xh(1)
+
+        def weights(a, G):
+            for tp in range(2):
+                turn_w(a, G, tp)
+                fetch_w(a, G, tp)
+
+        def feature_side(n):
+            turn_dz(n)
+            fetch_dz(n)
+
+        square(0)
+        neg_dz(0)
+        square(1)
+        neg_dz(1)
+        feature_side(0)
+        weights(0, 0)
+        quant_dzf(0)
+        quant_w(0, 0)
+        square(2)
+        feature_side(1)
+        square(3)
+        neg_dz(2)
+        weights(0, 1)
+        quant_dzf(1)
+        neg_dz(3)
+        quant_w(0, 1)
+        feature_side(2)
+        weave_dz(0, 0)
+        weights(1, 0)
+        quant_dzf(2)
+        weave_dz(0, 1)
+        quant_dzt(0, 0)
+        quant_w(1, 0)
+        weights(1, 1)
+        square(4)
+        quant_dzt(0, 1)
+        quant_w(1, 1)
+        feature_side(3)
+        square(5)
+        neg_dz(4)
+        quant_dzf(3)
+        neg_dz(5)
+        for n, a in ((0, 0), (0, 1), (1, 0), (1, 1), (2, 0)):
+            mm0(n, a)
+        square(6)
+        neg_dz(6)
+        square(7)
+        neg_dz(7)
+        turn_dz(4)
+        turn_dz(5)
+        drain("o0", 0, 0, False)
+        drain("o0", 0, 1, False)
+        fetch_dz(4)
+        fetch_dz(5)
+        mm0(2, 1)
+        mm0(3, 0)
+        weave_dz(1, 0)
+        quant_dzf(4)
+        quant_dzf(5)
+        turn_dz(6)
+        turn_dz(7)
+        drain("o0", 1, 0, False)
+        drain("o0", 1, 1, False)
+        store0(0)
+        mm0(3, 1)
+        fetch_dz(6)
+        fetch_dz(7)
+        weave_dz(1, 1)
+        quant_dzt(1, 0)
+        quant_dzf(6)
+        quant_dzf(7)
+        quant_dzt(1, 1)
+        for n, a in ((2, 0), (2, 1), (3, 0), (3, 1)):
+            drain("o0", n, a, False)
+        store0(1)
+        for c in range(3):
+            for g in range(2):
+                weave_x(c, g)
+            for g in range(2):
+                quant_x(c, g)
+        for n in range(4, 8):
+            for a in range(2):
+                mm0(n, a)
+                drain("o0", n, a, False)
+            if n % 2 == 1:
+                store0(n // 2)
+        for m in range(12):
+            for G in range(2):
+                mm1(m, G)
+                drain("o1", m, G, G == 1 and m >= 7)
+            if m >= 10:
+                store1(m, 1)
+            elif m % 2 == 1:
+                store1(m - 1, 2)

@@ -60,8 +60,8 @@ def tile_ryeelman_pa_v_kernel(
         def load_g(g, lo, hi):
             nc.sync.dma_start(out=g_sb[g][:, lo * H : hi * H], in_=rows4(grad_out, g)[:, lo * H : hi * H])
 
-        def load_w(a):
-            nc.sync.dma_start(out=w_sb[a][:], in_=rows4(W_ii, 1 + a))
+        def load_w(a, lo, hi):
+            nc.sync.dma_start(out=w_sb[a][:, lo * H : hi * H], in_=rows4(W_ii, 1 + a)[:, lo * H : hi * H])
 
         def load_xi(g):
             nc.sync.dma_start(out=xi_sb[g][:], in_=rows4(invariant_input, g))
@@ -96,9 +96,16 @@ def tile_ryeelman_pa_v_kernel(
                     nc.tensor.transpose(bank[:, 2 * G + u, :], words[:, 256 * G + u : 256 * (G + 1) : 2], ident[:])
             held["dzbank", n] = bank
 
-        def fetch_dz(n):
+        def move(on_vector, out, in_):
+            if on_vector:
+                nc.vector.tensor_copy(out=out, in_=in_)
+            else:
+                nc.scalar.copy(out=out, in_=in_)
+
+        def fetch_dz(n, on_vector):
             grouped = stage.tile([P, H], BF16, name="dzT", tag="dzT", align_bytes=64, bufs=3)
-            nc.scalar.copy(
+            move(
+                on_vector,
                 out=grouped[:].bitcast(F32).rearrange("q (G r u) -> q G r u", G=2, u=2),
                 in_=held["dzbank", n][:].rearrange("q (G u) r -> q G r u", G=2),
             )
@@ -119,11 +126,11 @@ def tile_ryeelman_pa_v_kernel(
                     nc.tensor.transpose(bank[:, 2 * t2 + u, :], words[:, c0 + u : c0 + 256 : 2], ident[:])
             held["wbank", a, G, tp] = bank
 
-        def fetch_w(a, G, tp):
+        def fetch_w(a, G, tp, on_vector):
             if tp == 0:
                 held["wT", a, G] = stage.tile([P, PACK * PASS], BF16, name="wT", tag="grouped", align_bytes=64)
             view = held["wT", a, G][:].bitcast(F32).rearrange("q (r s) -> q r s", s=8)
-            nc.scalar.copy(out=view[:, :, 4 * tp : 4 * tp + 4], in_=held["wbank", a, G, tp][:].rearrange("q s r -> q r s"))
+            move(on_vector, out=view[:, :, 4 * tp : 4 * tp + 4], in_=held["wbank", a, G, tp][:].rearrange("q s r -> q r s"))
 
         def quant_w(a, G):
             quant(wq[a, G], held["wT", a, G], E4)
@@ -193,111 +200,188 @@ def tile_ryeelman_pa_v_kernel(
                 in_=src.rearrange("p (t h) -> p t h", t=count),
             )
 
+        load_w(0, 0, 4)
+        turn_w(0, 0, 0)
+        fetch_w(0, 0, 0, True)
         load_y(0, 0, 1)
+        square(0)
         load_g(0, 0, 2)
         load_y(0, 1, 2)
-        load_w(0)
         load_y(1, 0, 2)
         load_g(0, 2, 4)
-        load_w(1)
+        load_w(1, 0, 4)
         load_y(2, 0, 2)
         load_g(1, 0, 4)
         load_y(3, 0, 2)
+        turn_w(0, 0, 1)
         load_xi(0)
-        load_xi(1)
-        load_xh(0)
-        load_xh(1)
-
-        def weights(a, G):
-            for tp in range(2):
-                turn_w(a, G, tp)
-                fetch_w(a, G, tp)
-
-        def feature_side(n):
-            turn_dz(n)
-            fetch_dz(n)
-
-        square(0)
+        turn_w(0, 1, 0)
         neg_dz(0)
+        load_xi(1)
+        fetch_w(0, 0, 1, False)
+        turn_w(0, 1, 1)
         square(1)
-        neg_dz(1)
-        feature_side(0)
-        weights(0, 0)
-        quant_dzf(0)
+        load_xh(0)
+        turn_dz(0)
+        fetch_w(0, 1, 0, True)
         quant_w(0, 0)
+        fetch_w(0, 1, 1, False)
+        neg_dz(1)
+        turn_dz(1)
         square(2)
-        feature_side(1)
-        square(3)
-        neg_dz(2)
-        weights(0, 1)
-        quant_dzf(1)
-        neg_dz(3)
+        load_xh(1)
         quant_w(0, 1)
-        feature_side(2)
+        neg_dz(2)
+        square(3)
+        turn_dz(2)
+        fetch_dz(0, False)
+        neg_dz(3)
+        fetch_dz(1, False)
+        fetch_dz(2, False)
+        quant_dzf(0)
+        turn_w(1, 0, 0)
+        quant_dzf(1)
         weave_dz(0, 0)
-        weights(1, 0)
-        quant_dzf(2)
+        turn_w(1, 0, 1)
+        fetch_w(1, 0, 0, False)
+        turn_w(1, 1, 0)
+        fetch_w(1, 0, 1, False)
         weave_dz(0, 1)
-        quant_dzt(0, 0)
-        quant_w(1, 0)
-        weights(1, 1)
+        turn_w(1, 1, 1)
         square(4)
+        quant_dzf(2)
+        turn_dz(3)
+        quant_dzt(0, 0)
+        fetch_w(1, 1, 0, False)
+        quant_w(1, 0)
+        fetch_w(1, 1, 1, False)
+        mm0(0, 0)
         quant_dzt(0, 1)
-        quant_w(1, 1)
-        feature_side(3)
         square(5)
         neg_dz(4)
-        quant_dzf(3)
-        neg_dz(5)
-        for n, a in ((0, 0), (0, 1), (1, 0), (1, 1), (2, 0)):
-            mm0(n, a)
+        fetch_dz(3, False)
+        quant_w(1, 1)
+        mm0(0, 1)
         square(6)
-        neg_dz(6)
+        neg_dz(5)
         square(7)
-        neg_dz(7)
-        turn_dz(4)
-        turn_dz(5)
+        mm0(1, 0)
+        quant_dzf(3)
+        neg_dz(6)
+        mm0(1, 1)
         drain("o0", 0, 0, False)
+        turn_dz(4)
         drain("o0", 0, 1, False)
-        fetch_dz(4)
-        fetch_dz(5)
-        mm0(2, 1)
-        mm0(3, 0)
-        weave_dz(1, 0)
-        quant_dzf(4)
-        quant_dzf(5)
-        turn_dz(6)
-        turn_dz(7)
+        neg_dz(7)
+        turn_dz(5)
         drain("o0", 1, 0, False)
+        mm0(2, 0)
         drain("o0", 1, 1, False)
         store0(0)
+        weave_x(0, 0)
+        mm0(2, 1)
+        fetch_dz(4, False)
+        turn_dz(6)
+        fetch_dz(5, False)
+        weave_x(0, 1)
+        mm0(3, 0)
+        drain("o0", 2, 0, False)
+        drain("o0", 2, 1, False)
         mm0(3, 1)
-        fetch_dz(6)
-        fetch_dz(7)
-        weave_dz(1, 1)
-        quant_dzt(1, 0)
-        quant_dzf(6)
-        quant_dzf(7)
-        quant_dzt(1, 1)
-        for n, a in ((2, 0), (2, 1), (3, 0), (3, 1)):
-            drain("o0", n, a, False)
+        fetch_dz(6, False)
+        quant_dzf(4)
+        turn_dz(7)
+        quant_dzf(5)
+        drain("o0", 3, 0, False)
+        weave_dz(1, 0)
+        mm0(4, 0)
+        drain("o0", 3, 1, False)
         store0(1)
-        for c in range(3):
-            for g in range(2):
-                weave_x(c, g)
-            for g in range(2):
-                quant_x(c, g)
-        for n in range(4, 8):
-            for a in range(2):
-                mm0(n, a)
-                drain("o0", n, a, False)
-            if n % 2 == 1:
-                store0(n // 2)
-        for m in range(12):
-            for G in range(2):
-                mm1(m, G)
-                drain("o1", m, G, G == 1 and m >= 7)
-            if m >= 10:
-                store1(m, 1)
-            elif m % 2 == 1:
-                store1(m - 1, 2)
+        mm0(4, 1)
+        fetch_dz(7, False)
+        quant_dzf(6)
+        mm0(5, 0)
+        drain("o0", 4, 0, False)
+        quant_x(0, 0)
+        mm0(5, 1)
+        drain("o0", 4, 1, False)
+        quant_dzf(7)
+        mm0(6, 0)
+        weave_dz(1, 1)
+        drain("o0", 5, 0, False)
+        mm0(6, 1)
+        drain("o0", 5, 1, False)
+        store0(2)
+        mm0(7, 0)
+        drain("o0", 6, 0, False)
+        quant_x(0, 1)
+        mm0(7, 1)
+        drain("o0", 6, 1, False)
+        quant_dzt(1, 0)
+        mm1(0, 0)
+        drain("o0", 7, 0, False)
+        quant_dzt(1, 1)
+        drain("o0", 7, 1, False)
+        store0(3)
+        weave_x(1, 0)
+        mm1(0, 1)
+        drain("o1", 0, 0, False)
+        mm1(1, 0)
+        drain("o1", 0, 1, False)
+        weave_x(1, 1)
+        mm1(1, 1)
+        drain("o1", 1, 0, False)
+        mm1(2, 0)
+        drain("o1", 1, 1, False)
+        store1(0, 2)
+        mm1(2, 1)
+        quant_x(1, 0)
+        drain("o1", 2, 0, False)
+        mm1(3, 0)
+        quant_x(1, 1)
+        drain("o1", 2, 1, False)
+        mm1(3, 1)
+        weave_x(2, 0)
+        drain("o1", 3, 0, False)
+        mm1(4, 0)
+        drain("o1", 3, 1, False)
+        store1(2, 2)
+        mm1(4, 1)
+        drain("o1", 4, 0, False)
+        weave_x(2, 1)
+        mm1(5, 0)
+        drain("o1", 4, 1, False)
+        mm1(5, 1)
+        drain("o1", 5, 0, False)
+        mm1(6, 0)
+        quant_x(2, 0)
+        drain("o1", 5, 1, False)
+        store1(4, 2)
+        mm1(6, 1)
+        quant_x(2, 1)
+        drain("o1", 6, 0, False)
+        mm1(7, 0)
+        drain("o1", 6, 1, False)
+        mm1(7, 1)
+        drain("o1", 7, 1, True)
+        drain("o1", 7, 0, False)
+        store1(6, 2)
+        mm1(8, 0)
+        drain("o1", 8, 0, False)
+        mm1(8, 1)
+        drain("o1", 8, 1, True)
+        mm1(9, 0)
+        drain("o1", 9, 0, False)
+        mm1(9, 1)
+        drain("o1", 9, 1, True)
+        store1(8, 2)
+        mm1(10, 0)
+        drain("o1", 10, 0, False)
+        mm1(10, 1)
+        drain("o1", 10, 1, True)
+        mm1(11, 0)
+        store1(10, 1)
+        drain("o1", 11, 0, False)
+        mm1(11, 1)
+        drain("o1", 11, 1, True)
+        store1(11, 1)

@@ -12,14 +12,22 @@ F32 = mybir.dt.float32
 BF16 = mybir.dt.bfloat16
 U32 = mybir.dt.uint32
 U8 = mybir.dt.uint8
-E4 = mybir.dt.float8_e4m3fn_x4
-E5 = mybir.dt.float8_e5m2_x4
+E4M3 = mybir.dt.float8_e4m3fn_x4
+E5M2 = mybir.dt.float8_e5m2_x4
 ALU = mybir.AluOpType
 ACT = mybir.ActivationFunctionType
 
 P = 128
 PACK = 4
 PASS = P * PACK
+PASS_WORDS = PASS // 2
+PER_BANK = PASS // P
+TURN_BANKS = 3
+SUM_BANKS = 5
+WOVEN_BUFS = 4
+TURNED_BUFS = 3
+RESULT_BUFS = 8
+SHARED_FROM = 7
 
 
 def tile_ryeelman_pa_v_kernel(
@@ -29,359 +37,218 @@ def tile_ryeelman_pa_v_kernel(
     nc = tc.nc
     with ExitStack() as ctx:
         keep = ctx.enter_context(tc.tile_pool(name="keep", bufs=1))
-        wide = ctx.enter_context(tc.tile_pool(name="wide", bufs=10))
-        stage = ctx.enter_context(tc.tile_pool(name="stage", bufs=4))
-        turn = ctx.enter_context(tc.psum_pool(name="turn", bufs=3))
-        sums = ctx.enter_context(tc.psum_pool(name="sums", bufs=5))
+        stage = ctx.enter_context(tc.tile_pool(name="stage", bufs=1))
+        turn = ctx.enter_context(tc.psum_pool(name="turn", bufs=TURN_BANKS))
+        sums = ctx.enter_context(tc.psum_pool(name="sums", bufs=SUM_BANKS))
         ctx.enter_context(tc.manual_schedule())
-
-        def rows4(t, g):
-            return t[g * PASS : (g + 1) * PASS, :].rearrange("(p j) w -> p (j w)", j=PACK)
-
-        def mx_tile(name, cols):
-            codes = keep.tile([P, cols], U32, name=name + "_codes", align_bytes=64)
-            scales = keep.tile([P, cols], U8, name=name + "_scales", align_bytes=64)
-            return codes, scales
 
         ident = keep.tile([P, P], F32, name="ident")
         make_identity(nc, ident[:])
 
-        y_sb = [wide.tile([P, 2 * H], F32, name="y%d" % n, tag="wide") for n in range(4)]
-        g_sb = [keep.tile([P, PACK * H], BF16, name="g%d" % g) for g in range(2)]
-        w_sb = [keep.tile([P, PACK * H], BF16, name="w%d" % a) for a in range(2)]
-        xi_sb = [keep.tile([P, PACK * I], BF16, name="xi%d" % g) for g in range(2)]
-        xh_sb = [keep.tile([P, PACK * H], BF16, name="xh%d" % g) for g in range(2)]
-        dz_sb = [keep.tile([P, PACK * H], BF16, name="dz%d" % g) for g in range(2)]
+        def four_rows(tensor, block):
+            return tensor[block * PASS : (block + 1) * PASS, :].rearrange("(p t) w -> p (t w)", t=PACK)
 
-        def load_y(n, lo, hi):
-            c0 = (n % 2) * 2 * H
-            nc.sync.dma_start(out=y_sb[n][:, lo * H : hi * H], in_=rows4(y, n // 2)[:, c0 + lo * H : c0 + hi * H])
+        def slots(lo, hi):
+            return slice(lo * H, hi * H)
 
-        def load_g(g, lo, hi):
-            nc.sync.dma_start(out=g_sb[g][:, lo * H : hi * H], in_=rows4(grad_out, g)[:, lo * H : hi * H])
+        def four_row_tiles(name, dtype, width):
+            return [keep.tile([P, PACK * width], dtype, name="%s%d" % (name, b)) for b in range(2)]
 
-        def load_w(a, lo, hi):
-            nc.sync.dma_start(out=w_sb[a][:, lo * H : hi * H], in_=rows4(W_ii, 1 + a)[:, lo * H : hi * H])
+        def mx_operand(name, columns):
+            codes = keep.tile([P, columns], U32, name=name + "_codes", align_bytes=64)
+            scales = keep.tile([P, columns], U8, name=name + "_scales", align_bytes=64)
+            return codes, scales
 
-        def load_xi(g):
-            nc.sync.dma_start(out=xi_sb[g][:], in_=rows4(invariant_input, g))
+        y_sb = four_row_tiles("y", F32, H)
+        grad_sb = four_row_tiles("grad", BF16, H)
+        w_sb = four_row_tiles("w", BF16, H)
+        input_sb = four_row_tiles("input", BF16, I)
+        hidden_sb = four_row_tiles("hidden", BF16, H)
+        neg_dz_sb = four_row_tiles("neg_dz", BF16, H)
 
-        def load_xh(g):
-            nc.sync.dma_start(out=xh_sb[g][:], in_=rows4(invariant_hidden, g))
+        dz_feat = [mx_operand("dz_feat%d" % n, 2 * P) for n in range(8)]
+        w_q = {(half, fp): mx_operand("w_q%d%d" % (half, fp), PASS) for half in range(2) for fp in range(2)}
+        dz_tok = {(tp, fp): mx_operand("dz_tok%d%d" % (tp, fp), PASS) for tp in range(2) for fp in range(2)}
+        inv_q = {(chunk, tp): mx_operand("inv_q%d%d" % (chunk, tp), PASS) for chunk in range(3) for tp in range(2)}
 
-        dzf = [mx_tile("dzf%d" % n, 2 * P) for n in range(8)]
-        wq = {(a, G): mx_tile("wq%d%d" % (a, G), PASS) for a in range(2) for G in range(2)}
-        dzt = {(g, G): mx_tile("dzt%d%d" % (g, G), PASS) for g in range(2) for G in range(2)}
-        xq = {(c, g): mx_tile("xq%d%d" % (c, g), PASS) for c in range(3) for g in range(2)}
-        held = {}
+        def load(tiles, tensor, b, columns, first_block=0):
+            nc.sync.dma_start(out=tiles[b][:, columns], in_=four_rows(tensor, first_block + b)[:, columns])
 
-        def y_unit(n):
-            return y_sb[n // 2][:, (n % 2) * H : (n % 2 + 1) * H]
+        def tile_of(tiles, n):
+            return tiles[n // PACK][:, slots(n % PACK, n % PACK + 1)]
 
         def square(n):
-            nc.scalar.activation(out=y_unit(n), in_=y_unit(n), func=ACT.Square)
+            nc.scalar.activation(out=tile_of(y_sb, n), in_=tile_of(y_sb, n), func=ACT.Square)
 
         def neg_dz(n):
-            cols = slice((n % 4) * H, (n % 4 + 1) * H)
             nc.vector.scalar_tensor_tensor(
-                out=dz_sb[n // 4][:, cols], in0=y_unit(n), scalar=1.0, in1=g_sb[n // 4][:, cols],
+                out=tile_of(neg_dz_sb, n), in0=tile_of(y_sb, n), scalar=1.0, in1=tile_of(grad_sb, n),
                 op0=ALU.subtract, op1=ALU.mult,
             )
 
+        def turn_words(words, starts):
+            bank = turn.tile([P, PER_BANK, P], F32, name="bank")
+            for s, start in enumerate(starts):
+                for u in range(2):
+                    nc.tensor.transpose(bank[:, 2 * s + u, :], words[:, start + u : start + PASS_WORDS : 2], ident[:])
+            return bank
+
         def turn_dz(n):
-            words = dz_sb[n // 4][:, (n % 4) * H : (n % 4 + 1) * H].bitcast(F32)
-            bank = turn.tile([P, 4, P], F32, name="bank", tag="bank")
-            for G in range(2):
-                for u in range(2):
-                    nc.tensor.transpose(bank[:, 2 * G + u, :], words[:, 256 * G + u : 256 * (G + 1) : 2], ident[:])
-            held["dzbank", n] = bank
+            return turn_words(tile_of(neg_dz_sb, n).bitcast(F32), [0, PASS_WORDS])
 
-        def move(on_vector, out, in_):
-            if on_vector:
-                nc.vector.tensor_copy(out=out, in_=in_)
-            else:
-                nc.scalar.copy(out=out, in_=in_)
-
-        def fetch_dz(n, on_vector):
-            grouped = stage.tile([P, H], BF16, name="dzT", tag="dzT", align_bytes=64, bufs=3)
-            move(
-                on_vector,
-                out=grouped[:].bitcast(F32).rearrange("q (G r u) -> q G r u", G=2, u=2),
-                in_=held["dzbank", n][:].rearrange("q (G u) r -> q G r u", G=2),
+        def fetch_dz(bank):
+            turned = stage.tile([P, H], BF16, name="turned", bufs=TURNED_BUFS, align_bytes=64)
+            nc.scalar.copy(
+                out=turned[:].bitcast(F32).rearrange("p (f r u) -> p f r u", f=2, u=2),
+                in_=bank[:].rearrange("p (f u) r -> p f r u", f=2),
             )
-            held["dzT", n] = grouped
+            return turned
 
-        def quant(dst, src, fmt):
-            nc.vector.quantize_mx(out=dst[0][:].bitcast(fmt), scales=dst[1][:], in_=src[:])
+        def woven_tile():
+            return stage.tile([P, PACK * PASS], BF16, name="woven", bufs=WOVEN_BUFS, align_bytes=64)
 
-        def quant_dzf(n):
-            quant(dzf[n], held["dzT", n], E5)
+        def turn_w(half, fp, pair):
+            starts = [(2 * pair + s) * (H // 2) + fp * PASS_WORDS for s in range(2)]
+            return turn_words(w_sb[half][:].bitcast(F32), starts)
 
-        def turn_w(a, G, tp):
-            words = w_sb[a][:].bitcast(F32)
-            bank = turn.tile([P, 4, P], F32, name="bank", tag="bank")
-            for t2 in range(2):
-                c0 = (2 * tp + t2) * 512 + 256 * G
-                for u in range(2):
-                    nc.tensor.transpose(bank[:, 2 * t2 + u, :], words[:, c0 + u : c0 + 256 : 2], ident[:])
-            held["wbank", a, G, tp] = bank
+        def fetch_w(copy, woven, pair, bank):
+            words = woven[:].bitcast(F32).rearrange("p (r s) -> p r s", s=2 * PACK)
+            copy(out=words[:, :, PER_BANK * pair : PER_BANK * (pair + 1)], in_=bank[:].rearrange("p s r -> p r s"))
 
-        def fetch_w(a, G, tp, on_vector):
-            if tp == 0:
-                held["wT", a, G] = stage.tile([P, PACK * PASS], BF16, name="wT", tag="grouped", align_bytes=64)
-            view = held["wT", a, G][:].bitcast(F32).rearrange("q (r s) -> q r s", s=8)
-            move(on_vector, out=view[:, :, 4 * tp : 4 * tp + 4], in_=held["wbank", a, G, tp][:].rearrange("q s r -> q r s"))
-
-        def quant_w(a, G):
-            quant(wq[a, G], held["wT", a, G], E4)
-
-        def weave(key, src):
-            grouped = stage.tile([P, PACK * PASS], BF16, name="woven", tag="grouped", align_bytes=64)
+        def weave(tile, first_column):
+            rows = tile[:].rearrange("p (t w) -> p t w", t=PACK)[:, :, first_column : first_column + PASS]
+            woven = woven_tile()
             nc.vector.tensor_copy(
-                out=grouped[:].rearrange("p (c i t) -> p c t i", i=4, t=PACK),
-                in_=src.rearrange("p t (c i) -> p c t i", i=4),
+                out=woven[:].rearrange("p (c i t) -> p c t i", i=4, t=PACK),
+                in_=rows.rearrange("p t (c i) -> p c t i", i=4),
             )
-            held[key] = grouped
+            return woven
 
-        def weave_dz(g, G):
-            weave(("dzw", g, G), dz_sb[g][:].rearrange("p (t h) -> p t h", t=PACK)[:, :, G * PASS : (G + 1) * PASS])
+        def quantize(operand, values, fmt):
+            codes, scales = operand
+            nc.vector.quantize_mx(out=codes[:].bitcast(fmt), scales=scales[:], in_=values[:])
 
-        def quant_dzt(g, G):
-            quant(dzt[g, G], held["dzw", g, G], E5)
-
-        def weave_x(c, g):
-            if c == 0:
-                src = xi_sb[g][:].rearrange("p (t f) -> p t f", t=PACK)
-            else:
-                src = xh_sb[g][:].rearrange("p (t f) -> p t f", t=PACK)[:, :, (c - 1) * PASS : c * PASS]
-            weave(("xw", c, g), src)
-
-        def quant_x(c, g):
-            quant(xq[c, g], held["xw", c, g], E4)
-
-        def product(key, lhs, lhs_fmt, rhs, rhs_fmt):
-            acc = sums.tile([P, PASS], F32, name="acc", tag="acc")
+        def two_passes(stationary, columns, stationary_fmt, moving, moving_fmt):
+            acc = sums.tile([P, PASS], F32, name="acc")
             for k in range(2):
-                (lc, ls), cols = lhs[k]
-                rc, rs = rhs[k]
                 nc.tensor.matmul_mx(
-                    out=acc[:], lhsT=lc[:, cols].bitcast(lhs_fmt), lhsT_scale=ls[:, cols],
-                    rhs=rc[:].bitcast(rhs_fmt), rhs_scale=rs[:], start=(k == 0), stop=(k == 1),
+                    out=acc[:],
+                    lhsT=stationary[k][0][:, columns[k]].bitcast(stationary_fmt),
+                    lhsT_scale=stationary[k][1][:, columns[k]],
+                    rhs=moving[k][0][:].bitcast(moving_fmt),
+                    rhs_scale=moving[k][1][:],
+                    start=(k == 0),
+                    stop=(k == 1),
                 )
-            held[key] = acc
+            return acc
 
-        def mm0(n, a):
-            product(("acc0", n, a), [(dzf[n], slice(G * P, (G + 1) * P)) for G in range(2)], E5,
-                    [wq[a, G] for G in range(2)], E4)
+        def sums_0(n):
+            columns = [slice(fp * P, (fp + 1) * P) for fp in range(2)]
+            return [
+                two_passes([dz_feat[n]] * 2, columns, E5M2, [w_q[half, fp] for fp in range(2)], E4M3)
+                for half in range(2)
+            ]
 
-        def mm1(m, G):
-            cols = slice((m % 4) * P, (m % 4 + 1) * P)
-            product(("acc1", m, G), [(xq[m // 4, g], cols) for g in range(2)], E4, [dzt[g, G] for g in range(2)], E5)
-
-        def drain(name, n, half, on_vector):
-            if (name, n // 2) not in held:
-                held[name, n // 2] = wide.tile([P, 2 * H], F32, name=name, tag="wide")
-            c0 = (n % 2) * H + half * PASS
-            dst = held[name, n // 2][:, c0 : c0 + PASS]
-            acc = held["acc" + name[-1], n, half]
-            if on_vector:
-                nc.vector.tensor_scalar(out=dst, in0=acc[:], scalar1=-1.0, scalar2=None, op0=ALU.mult)
-            else:
-                nc.scalar.activation(out=dst, in_=acc[:], func=ACT.Copy, scale=-1.0)
-
-        def store0(pair):
-            c0 = (pair % 2) * 2 * H
-            nc.sync.dma_start(out=rows4(out_0, pair // 2)[:, c0 : c0 + 2 * H], in_=held["o0", pair][:])
-
-        def store1(m, count):
-            src = held["o1", m // 2][:, (m % 2) * H : (m % 2 + count) * H]
-            nc.sync.dma_start(
-                out=out_1[m * P : (m + count) * P, :].rearrange("(t p) h -> p t h", p=P),
-                in_=src.rearrange("p (t h) -> p t h", t=count),
+        def sum_1(m, fp):
+            columns = [slice((m % PACK) * P, (m % PACK + 1) * P)] * 2
+            return two_passes(
+                [inv_q[m // PACK, tp] for tp in range(2)], columns, E4M3, [dz_tok[tp, fp] for tp in range(2)], E5M2
             )
 
-        load_w(0, 0, 4)
-        turn_w(0, 0, 0)
-        fetch_w(0, 0, 0, True)
-        load_y(0, 0, 1)
-        square(0)
-        load_g(0, 0, 2)
-        load_y(0, 1, 2)
-        load_y(1, 0, 2)
-        load_g(0, 2, 4)
-        load_w(1, 0, 4)
-        load_y(2, 0, 2)
-        load_g(1, 0, 4)
-        load_y(3, 0, 2)
-        turn_w(0, 0, 1)
-        load_xi(0)
-        turn_w(0, 1, 0)
-        neg_dz(0)
-        load_xi(1)
-        fetch_w(0, 0, 1, False)
-        turn_w(0, 1, 1)
-        square(1)
-        load_xh(0)
-        turn_dz(0)
-        fetch_w(0, 1, 0, True)
-        quant_w(0, 0)
-        fetch_w(0, 1, 1, False)
-        neg_dz(1)
-        turn_dz(1)
-        square(2)
-        load_xh(1)
-        quant_w(0, 1)
-        neg_dz(2)
-        square(3)
-        turn_dz(2)
-        fetch_dz(0, False)
-        neg_dz(3)
-        fetch_dz(1, False)
-        fetch_dz(2, False)
-        quant_dzf(0)
-        turn_w(1, 0, 0)
-        quant_dzf(1)
-        weave_dz(0, 0)
-        turn_w(1, 0, 1)
-        fetch_w(1, 0, 0, False)
-        turn_w(1, 1, 0)
-        fetch_w(1, 0, 1, False)
-        weave_dz(0, 1)
-        turn_w(1, 1, 1)
-        square(4)
-        quant_dzf(2)
-        turn_dz(3)
-        quant_dzt(0, 0)
-        fetch_w(1, 1, 0, False)
-        quant_w(1, 0)
-        fetch_w(1, 1, 1, False)
-        mm0(0, 0)
-        quant_dzt(0, 1)
-        square(5)
-        neg_dz(4)
-        fetch_dz(3, False)
-        quant_w(1, 1)
-        mm0(0, 1)
-        square(6)
-        neg_dz(5)
-        square(7)
-        mm0(1, 0)
-        quant_dzf(3)
-        neg_dz(6)
-        mm0(1, 1)
-        drain("o0", 0, 0, False)
-        turn_dz(4)
-        drain("o0", 0, 1, False)
-        neg_dz(7)
-        turn_dz(5)
-        drain("o0", 1, 0, False)
-        mm0(2, 0)
-        drain("o0", 1, 1, False)
-        store0(0)
-        weave_x(0, 0)
-        mm0(2, 1)
-        fetch_dz(4, False)
-        turn_dz(6)
-        fetch_dz(5, False)
-        weave_x(0, 1)
-        mm0(3, 0)
-        drain("o0", 2, 0, False)
-        drain("o0", 2, 1, False)
-        mm0(3, 1)
-        fetch_dz(6, False)
-        quant_dzf(4)
-        turn_dz(7)
-        quant_dzf(5)
-        drain("o0", 3, 0, False)
-        weave_dz(1, 0)
-        mm0(4, 0)
-        drain("o0", 3, 1, False)
-        store0(1)
-        mm0(4, 1)
-        fetch_dz(7, False)
-        quant_dzf(6)
-        mm0(5, 0)
-        drain("o0", 4, 0, False)
-        quant_x(0, 0)
-        mm0(5, 1)
-        drain("o0", 4, 1, False)
-        quant_dzf(7)
-        mm0(6, 0)
-        weave_dz(1, 1)
-        drain("o0", 5, 0, False)
-        mm0(6, 1)
-        drain("o0", 5, 1, False)
-        store0(2)
-        mm0(7, 0)
-        drain("o0", 6, 0, False)
-        quant_x(0, 1)
-        mm0(7, 1)
-        drain("o0", 6, 1, False)
-        quant_dzt(1, 0)
-        mm1(0, 0)
-        drain("o0", 7, 0, False)
-        quant_dzt(1, 1)
-        drain("o0", 7, 1, False)
-        store0(3)
-        weave_x(1, 0)
-        mm1(0, 1)
-        drain("o1", 0, 0, False)
-        mm1(1, 0)
-        drain("o1", 0, 1, False)
-        weave_x(1, 1)
-        mm1(1, 1)
-        drain("o1", 1, 0, False)
-        mm1(2, 0)
-        drain("o1", 1, 1, False)
-        store1(0, 2)
-        mm1(2, 1)
-        quant_x(1, 0)
-        drain("o1", 2, 0, False)
-        mm1(3, 0)
-        quant_x(1, 1)
-        drain("o1", 2, 1, False)
-        mm1(3, 1)
-        weave_x(2, 0)
-        drain("o1", 3, 0, False)
-        mm1(4, 0)
-        drain("o1", 3, 1, False)
-        store1(2, 2)
-        mm1(4, 1)
-        drain("o1", 4, 0, False)
-        weave_x(2, 1)
-        mm1(5, 0)
-        drain("o1", 4, 1, False)
-        mm1(5, 1)
-        drain("o1", 5, 0, False)
-        mm1(6, 0)
-        quant_x(2, 0)
-        drain("o1", 5, 1, False)
-        store1(4, 2)
-        mm1(6, 1)
-        quant_x(2, 1)
-        drain("o1", 6, 0, False)
-        mm1(7, 0)
-        drain("o1", 6, 1, False)
-        mm1(7, 1)
-        drain("o1", 7, 1, True)
-        drain("o1", 7, 0, False)
-        store1(6, 2)
-        mm1(8, 0)
-        drain("o1", 8, 0, False)
-        mm1(8, 1)
-        drain("o1", 8, 1, True)
-        mm1(9, 0)
-        drain("o1", 9, 0, False)
-        mm1(9, 1)
-        drain("o1", 9, 1, True)
-        store1(8, 2)
-        mm1(10, 0)
-        drain("o1", 10, 0, False)
-        mm1(10, 1)
-        drain("o1", 10, 1, True)
-        mm1(11, 0)
-        store1(10, 1)
-        drain("o1", 11, 0, False)
-        mm1(11, 1)
-        drain("o1", 11, 1, True)
-        store1(11, 1)
+        def result_tile():
+            return stage.tile([P, H], F32, name="result", bufs=RESULT_BUFS)
+
+        def negate_out(result, part, acc, on_vector):
+            target = result[:, part * PASS : (part + 1) * PASS]
+            if on_vector:
+                nc.vector.tensor_scalar(out=target, in0=acc[:], scalar1=-1.0, scalar2=None, op0=ALU.mult)
+            else:
+                nc.scalar.activation(out=target, in_=acc[:], func=ACT.Copy, scale=-1.0)
+
+        def finish_0(n, accs):
+            result = result_tile()
+            for half in range(2):
+                negate_out(result, half, accs[half], False)
+            nc.sync.dma_start(out=four_rows(out_0, n // PACK)[:, slots(n % PACK, n % PACK + 1)], in_=result[:])
+
+        load(w_sb, W_ii, 0, slots(0, 4), first_block=1)
+        load(y_sb, y, 0, slots(0, 1))
+        load(grad_sb, grad_out, 0, slots(0, 2))
+        load(y_sb, y, 0, slots(1, 2))
+        load(y_sb, y, 0, slots(2, 4))
+        load(grad_sb, grad_out, 0, slots(2, 4))
+        load(w_sb, W_ii, 1, slots(0, 4), first_block=1)
+        load(y_sb, y, 1, slots(0, 2))
+        load(grad_sb, grad_out, 1, slots(0, 4))
+        load(y_sb, y, 1, slots(2, 4))
+        for tiles, tensor, width in ((input_sb, invariant_input, I), (hidden_sb, invariant_hidden, H)):
+            for tp in range(2):
+                load(tiles, tensor, tp, slice(0, PACK * width))
+
+        w_woven = []
+        for fp in range(2):
+            banks = [turn_w(0, fp, pair) for pair in range(2)]
+            square(fp)
+            w_woven.append(woven_tile())
+            fetch_w(nc.vector.tensor_copy, w_woven[fp], 0, banks[0])
+            fetch_w(nc.scalar.copy, w_woven[fp], 1, banks[1])
+            if fp == 1:
+                quantize(w_q[0, 0], w_woven[0], E4M3)
+            neg_dz(fp)
+        quantize(w_q[0, 1], w_woven[1], E4M3)
+
+        for n in (2, 3):
+            square(n)
+            neg_dz(n)
+        turned = [fetch_dz(turn_dz(n)) for n in range(TURN_BANKS)]
+        for n in (0, 1):
+            quantize(dz_feat[n], turned[n], E5M2)
+        dz_woven = [weave(neg_dz_sb[0], fp * PASS) for fp in range(2)]
+        quantize(dz_feat[2], turned[2], E5M2)
+
+        for fp in range(2):
+            woven = woven_tile()
+            for pair in range(2):
+                fetch_w(nc.scalar.copy, woven, pair, turn_w(1, fp, pair))
+            square(4 + fp)
+            quantize(dz_tok[0, fp], dz_woven[fp], E5M2)
+            quantize(w_q[1, fp], woven, E4M3)
+            neg_dz(4 + fp)
+        quantize(dz_feat[3], fetch_dz(turn_dz(3)), E5M2)
+
+        for n in (6, 7):
+            square(n)
+            neg_dz(n)
+
+        accs = [sums_0(n) for n in (0, 1)]
+        banks, input_woven = [], []
+        for n in (0, 1):
+            banks.append(turn_dz(4 + n))
+            finish_0(n, accs[n])
+            input_woven.append(weave(input_sb[n], 0))
+        for n in (0, 1):
+            quantize(dz_feat[4 + n], fetch_dz(banks[n]), E5M2)
+        dz_woven = []
+        for n in (0, 1):
+            pending = sums_0(2 + n)
+            bank = turn_dz(6 + n)
+            finish_0(2 + n, pending)
+            last_turned = fetch_dz(bank)
+            dz_woven.append(weave(neg_dz_sb[1], n * PASS))
+            quantize(dz_feat[6 + n], last_turned, E5M2)
+            quantize(inv_q[0, n], input_woven[n], E4M3)
+        for fp in range(2):
+            quantize(dz_tok[1, fp], dz_woven[fp], E5M2)
+
+        for chunk in (1, 2):
+            hidden_woven = [weave(hidden_sb[tp], (chunk - 1) * PASS) for tp in range(2)]
+            for tp in range(2):
+                quantize(inv_q[chunk, tp], hidden_woven[tp], E4M3)
+
+        for n in range(4, 8):
+            finish_0(n, sums_0(n))
+        for m in range(K // P):
+            result = result_tile()
+            for fp in range(2):
+                negate_out(result, fp, sum_1(m, fp), fp == 1 and m >= SHARED_FROM)
+            nc.sync.dma_start(out=out_1[m * P : (m + 1) * P, :], in_=result[:])

@@ -81,20 +81,25 @@ def tile_ryeelman_pa_v_kernel(
             nc.scalar.activation(out=tile_of(y_sb, n), in_=tile_of(y_sb, n), func=ACT.Square)
 
         def neg_dz(n):
-            nc.vector.scalar_tensor_tensor(
-                out=tile_of(neg_dz_sb, n), in0=tile_of(y_sb, n), scalar=1.0, in1=tile_of(grad_sb, n),
-                op0=ALU.subtract, op1=ALU.mult,
-            )
+            for u in range(2):
+                nc.vector.scalar_tensor_tensor(
+                    out=tile_of(neg_dz_sb, n).rearrange("p (u w e) -> p u w e", u=2, e=2)[:, u],
+                    in0=tile_of(y_sb, n).rearrange("p (w u e) -> p u w e", u=2, e=2)[:, u],
+                    scalar=1.0,
+                    in1=tile_of(grad_sb, n).rearrange("p (w u e) -> p u w e", u=2, e=2)[:, u],
+                    op0=ALU.subtract,
+                    op1=ALU.mult,
+                )
 
-        def turn_words(words, starts):
+        def turn_words(words, windows):
             bank = turn.tile([P, PER_BANK, P], F32, name="bank")
-            for s, start in enumerate(starts):
-                for u in range(2):
-                    nc.tensor.transpose(bank[:, 2 * s + u, :], words[:, start + u : start + PASS_WORDS : 2], ident[:])
+            for s, window in enumerate(windows):
+                nc.tensor.transpose(bank[:, s, :], words[:, window], ident[:])
             return bank
 
         def turn_dz(n):
-            return turn_words(tile_of(neg_dz_sb, n).bitcast(F32), [0, PASS_WORDS])
+            starts = [u * PASS_WORDS + fp * P for fp in range(2) for u in range(2)]
+            return turn_words(tile_of(neg_dz_sb, n).bitcast(F32), [slice(s, s + P) for s in starts])
 
         def fetch_dz(bank):
             turned = stage.tile([P, H], BF16, name="turned", bufs=TURNED_BUFS, align_bytes=64)
@@ -109,7 +114,8 @@ def tile_ryeelman_pa_v_kernel(
 
         def turn_w(half, fp, pair):
             starts = [(2 * pair + s) * (H // 2) + fp * PASS_WORDS for s in range(2)]
-            return turn_words(w_sb[half][:].bitcast(F32), starts)
+            windows = [slice(start + u, start + PASS_WORDS, 2) for start in starts for u in range(2)]
+            return turn_words(w_sb[half][:].bitcast(F32), windows)
 
         def fetch_w(copy, woven, pair, bank):
             words = woven[:].bitcast(F32).rearrange("p (r s) -> p r s", s=2 * PACK)
@@ -122,6 +128,12 @@ def tile_ryeelman_pa_v_kernel(
                 out=woven[:].rearrange("p (c i t) -> p c t i", i=4, t=PACK),
                 in_=rows.rearrange("p t (c i) -> p c t i", i=4),
             )
+            return woven
+
+        def weave_dz(tp, fp):
+            rows = neg_dz_sb[tp][:].rearrange("p (t u f c i) -> p f u c t i", t=PACK, u=2, f=2, i=4)[:, fp]
+            woven = woven_tile()
+            nc.vector.tensor_copy(out=woven[:].rearrange("p (u c i t) -> p u c t i", u=2, i=4, t=PACK), in_=rows)
             return woven
 
         def quantize(operand, values, fmt):
@@ -158,17 +170,16 @@ def tile_ryeelman_pa_v_kernel(
         def result_tile():
             return stage.tile([P, H], F32, name="result", bufs=RESULT_BUFS)
 
-        def negate_out(result, part, acc, on_vector):
-            target = result[:, part * PASS : (part + 1) * PASS]
+        def negate(target, source, on_vector):
             if on_vector:
-                nc.vector.tensor_scalar(out=target, in0=acc[:], scalar1=-1.0, scalar2=None, op0=ALU.mult)
+                nc.vector.tensor_scalar(out=target, in0=source, scalar1=-1.0, scalar2=None, op0=ALU.mult)
             else:
-                nc.scalar.activation(out=target, in_=acc[:], func=ACT.Copy, scale=-1.0)
+                nc.scalar.activation(out=target, in_=source, func=ACT.Copy, scale=-1.0)
 
         def finish_0(n, accs):
             result = result_tile()
             for half in range(2):
-                negate_out(result, half, accs[half], False)
+                negate(result[:, half * PASS : (half + 1) * PASS], accs[half][:], False)
             nc.sync.dma_start(out=four_rows(out_0, n // PACK)[:, slots(n % PACK, n % PACK + 1)], in_=result[:])
 
         load(w_sb, W_ii, 0, slots(0, 4), first_block=1)
@@ -203,7 +214,7 @@ def tile_ryeelman_pa_v_kernel(
         turned = [fetch_dz(turn_dz(n)) for n in range(TURN_BANKS)]
         for n in (0, 1):
             quantize(dz_feat[n], turned[n], E5M2)
-        dz_woven = [weave(neg_dz_sb[0], fp * PASS) for fp in range(2)]
+        dz_woven = [weave_dz(0, fp) for fp in range(2)]
         quantize(dz_feat[2], turned[2], E5M2)
 
         for fp in range(2):
@@ -234,7 +245,7 @@ def tile_ryeelman_pa_v_kernel(
             bank = turn_dz(6 + n)
             finish_0(2 + n, pending)
             last_turned = fetch_dz(bank)
-            dz_woven.append(weave(neg_dz_sb[1], n * PASS))
+            dz_woven.append(weave_dz(1, n))
             quantize(dz_feat[6 + n], last_turned, E5M2)
             quantize(inv_q[0, n], input_woven[n], E4M3)
         for fp in range(2):
@@ -247,8 +258,18 @@ def tile_ryeelman_pa_v_kernel(
 
         for n in range(4, 8):
             finish_0(n, sums_0(n))
-        for m in range(K // P):
+        last = K // P - 1
+        for m in range(last + 1):
             result = result_tile()
+            rows = slice(m * P, (m + 1) * P)
             for fp in range(2):
-                negate_out(result, fp, sum_1(m, fp), fp == 1 and m >= SHARED_FROM)
-            nc.sync.dma_start(out=out_1[m * P : (m + 1) * P, :], in_=result[:])
+                columns = slice(fp * PASS, (fp + 1) * PASS)
+                negate(
+                    result[:, columns].rearrange("p (w u e) -> p w u e", u=2, e=2),
+                    sum_1(m, fp)[:].rearrange("p (u w e) -> p w u e", u=2, e=2),
+                    fp == 1 and m >= SHARED_FROM,
+                )
+                if m == last:
+                    nc.sync.dma_start(out=out_1[rows, columns], in_=result[:, columns])
+            if m < last:
+                nc.sync.dma_start(out=out_1[rows, :], in_=result[:])

from contextlib import ExitStack

import concourse.mybir as mybir
from concourse.masks import make_identity

B, I, H = 1024, 512, 1024
K = I + H
FLOPS = 2 * B * H * H + 2 * B * K * H
BYTES = B * K * 2 + H * H * 2 + B * H * 4 + B * H * 2 + B * H * 4 + K * H * 4

F32 = mybir.dt.float32
BF16 = mybir.dt.bfloat16
U32 = mybir.dt.uint32
U8 = mybir.dt.uint8
E4M3 = mybir.dt.float8_e4m3fn_x4
E5M2 = mybir.dt.float8_e5m2_x4
ALU = mybir.AluOpType
ACT = mybir.ActivationFunctionType

P = 128
PACK = 4
PASS = P * PACK
PASS_WORDS = PASS // 2
PER_BANK = PASS // P
TURN_BANKS = 3
SUM_BANKS = 5
WOVEN_BUFS = 4
TURNED_BUFS = 3
RESULT_BUFS = 8
SHARED_FROM = 7


def tile_ryeelman_pa_v_kernel(
    tc, invariant_input, equivariant_input, invariant_hidden, equivariant_hidden,
    W_left, W_right, W_ii, b_ii, y, grad_out, out_0, out_1,
):
    nc = tc.nc
    with ExitStack() as ctx:
        keep = ctx.enter_context(tc.tile_pool(name="keep", bufs=1))
        stage = ctx.enter_context(tc.tile_pool(name="stage", bufs=1))
        turn = ctx.enter_context(tc.psum_pool(name="turn", bufs=TURN_BANKS))
        sums = ctx.enter_context(tc.psum_pool(name="sums", bufs=SUM_BANKS))
        ctx.enter_context(tc.manual_schedule())

        ident = keep.tile([P, P], F32, name="ident")
        make_identity(nc, ident[:])

        def four_rows(tensor, block):
            return tensor[block * PASS : (block + 1) * PASS, :].rearrange("(p t) w -> p (t w)", t=PACK)

        def slots(lo, hi):
            return slice(lo * H, hi * H)

        def four_row_tiles(name, dtype, width):
            return [keep.tile([P, PACK * width], dtype, name="%s%d" % (name, b)) for b in range(2)]

        def mx_operand(name, columns):
            codes = keep.tile([P, columns], U32, name=name + "_codes", align_bytes=64)
            scales = keep.tile([P, columns], U8, name=name + "_scales", align_bytes=64)
            return codes, scales

        y_sb = four_row_tiles("y", F32, H)
        grad_sb = four_row_tiles("grad", BF16, H)
        w_sb = four_row_tiles("w", BF16, H)
        input_sb = four_row_tiles("input", BF16, I)
        hidden_sb = four_row_tiles("hidden", BF16, H)
        neg_dz_sb = four_row_tiles("neg_dz", BF16, H)

        dz_feat = [mx_operand("dz_feat%d" % n, 2 * P) for n in range(8)]
        w_q = {(half, fp): mx_operand("w_q%d%d" % (half, fp), PASS) for half in range(2) for fp in range(2)}
        dz_tok = {(tp, fp): mx_operand("dz_tok%d%d" % (tp, fp), PASS) for tp in range(2) for fp in range(2)}
        inv_q = {(chunk, tp): mx_operand("inv_q%d%d" % (chunk, tp), PASS) for chunk in range(3) for tp in range(2)}

        def load(tiles, tensor, b, columns, first_block=0):
            nc.sync.dma_start(out=tiles[b][:, columns], in_=four_rows(tensor, first_block + b)[:, columns])

        def tile_of(tiles, n):
            return tiles[n // PACK][:, slots(n % PACK, n % PACK + 1)]

        def square(n):
            nc.scalar.activation(out=tile_of(y_sb, n), in_=tile_of(y_sb, n), func=ACT.Square)

        def neg_dz(n):
            for u in range(2):
                nc.vector.scalar_tensor_tensor(
                    out=tile_of(neg_dz_sb, n).rearrange("p (u w e) -> p u w e", u=2, e=2)[:, u],
                    in0=tile_of(y_sb, n).rearrange("p (w u e) -> p u w e", u=2, e=2)[:, u],
                    scalar=1.0,
                    in1=tile_of(grad_sb, n).rearrange("p (w u e) -> p u w e", u=2, e=2)[:, u],
                    op0=ALU.subtract,
                    op1=ALU.mult,
                )

        def turn_words(words, windows):
            bank = turn.tile([P, PER_BANK, P], F32, name="bank")
            for s, window in enumerate(windows):
                nc.tensor.transpose(bank[:, s, :], words[:, window], ident[:])
            return bank

        def turn_dz(n):
            starts = [u * PASS_WORDS + fp * P for fp in range(2) for u in range(2)]
            return turn_words(tile_of(neg_dz_sb, n).bitcast(F32), [slice(s, s + P) for s in starts])

        def fetch_dz(bank):
            turned = stage.tile([P, H], BF16, name="turned", bufs=TURNED_BUFS, align_bytes=64)
            nc.scalar.copy(
                out=turned[:].bitcast(F32).rearrange("p (f r u) -> p f r u", f=2, u=2),
                in_=bank[:].rearrange("p (f u) r -> p f r u", f=2),
            )
            return turned

        def woven_tile():
            return stage.tile([P, PACK * PASS], BF16, name="woven", bufs=WOVEN_BUFS, align_bytes=64)

        def turn_w(half, fp, pair):
            starts = [(2 * pair + s) * (H // 2) + fp * PASS_WORDS for s in range(2)]
            windows = [slice(start + u, start + PASS_WORDS, 2) for start in starts for u in range(2)]
            return turn_words(w_sb[half][:].bitcast(F32), windows)

        def fetch_w(copy, woven, pair, bank):
            words = woven[:].bitcast(F32).rearrange("p (r s) -> p r s", s=2 * PACK)
            copy(out=words[:, :, PER_BANK * pair : PER_BANK * (pair + 1)], in_=bank[:].rearrange("p s r -> p r s"))

        def weave(tile, first_column):
            rows = tile[:].rearrange("p (t w) -> p t w", t=PACK)[:, :, first_column : first_column + PASS]
            woven = woven_tile()
            nc.vector.tensor_copy(
                out=woven[:].rearrange("p (c i t) -> p c t i", i=4, t=PACK),
                in_=rows.rearrange("p t (c i) -> p c t i", i=4),
            )
            return woven

        def weave_dz(tp, fp):
            rows = neg_dz_sb[tp][:].rearrange("p (t u f c i) -> p f u c t i", t=PACK, u=2, f=2, i=4)[:, fp]
            woven = woven_tile()
            nc.vector.tensor_copy(out=woven[:].rearrange("p (u c i t) -> p u c t i", u=2, i=4, t=PACK), in_=rows)
            return woven

        def quantize(operand, values, fmt):
            codes, scales = operand
            nc.vector.quantize_mx(out=codes[:].bitcast(fmt), scales=scales[:], in_=values[:])

        def two_passes(stationary, columns, stationary_fmt, moving, moving_fmt):
            acc = sums.tile([P, PASS], F32, name="acc")
            for k in range(2):
                nc.tensor.matmul_mx(
                    out=acc[:],
                    lhsT=stationary[k][0][:, columns[k]].bitcast(stationary_fmt),
                    lhsT_scale=stationary[k][1][:, columns[k]],
                    rhs=moving[k][0][:].bitcast(moving_fmt),
                    rhs_scale=moving[k][1][:],
                    start=(k == 0),
                    stop=(k == 1),
                )
            return acc

        def sums_0(n):
            columns = [slice(fp * P, (fp + 1) * P) for fp in range(2)]
            return [
                two_passes([dz_feat[n]] * 2, columns, E5M2, [w_q[half, fp] for fp in range(2)], E4M3)
                for half in range(2)
            ]

        def sum_1(m, fp):
            columns = [slice((m % PACK) * P, (m % PACK + 1) * P)] * 2
            return two_passes(
                [inv_q[m // PACK, tp] for tp in range(2)], columns, E4M3, [dz_tok[tp, fp] for tp in range(2)], E5M2
            )

        def result_tile():
            return stage.tile([P, H], F32, name="result", bufs=RESULT_BUFS)

        def negate(target, source, on_vector):
            if on_vector:
                nc.vector.tensor_scalar(out=target, in0=source, scalar1=-1.0, scalar2=None, op0=ALU.mult)
            else:
                nc.scalar.activation(out=target, in_=source, func=ACT.Copy, scale=-1.0)

        def finish_0(n, accs):
            result = result_tile()
            for half in range(2):
                negate(result[:, half * PASS : (half + 1) * PASS], accs[half][:], False)
            nc.sync.dma_start(out=four_rows(out_0, n // PACK)[:, slots(n % PACK, n % PACK + 1)], in_=result[:])

        load(w_sb, W_ii, 0, slots(0, 4), first_block=1)
        load(y_sb, y, 0, slots(0, 1))
        load(grad_sb, grad_out, 0, slots(0, 2))
        load(y_sb, y, 0, slots(1, 2))
        load(y_sb, y, 0, slots(2, 4))
        load(grad_sb, grad_out, 0, slots(2, 4))
        load(w_sb, W_ii, 1, slots(0, 4), first_block=1)
        load(y_sb, y, 1, slots(0, 2))
        load(grad_sb, grad_out, 1, slots(0, 4))
        load(y_sb, y, 1, slots(2, 4))
        for tiles, tensor, width in ((input_sb, invariant_input, I), (hidden_sb, invariant_hidden, H)):
            for tp in range(2):
                load(tiles, tensor, tp, slice(0, PACK * width))

        w_woven = []
        for fp in range(2):
            banks = [turn_w(0, fp, pair) for pair in range(2)]
            square(fp)
            w_woven.append(woven_tile())
            fetch_w(nc.vector.tensor_copy, w_woven[fp], 0, banks[0])
            fetch_w(nc.scalar.copy, w_woven[fp], 1, banks[1])
            if fp == 1:
                quantize(w_q[0, 0], w_woven[0], E4M3)
            neg_dz(fp)
        quantize(w_q[0, 1], w_woven[1], E4M3)

        for n in (2, 3):
            square(n)
            neg_dz(n)
        turned = [fetch_dz(turn_dz(n)) for n in range(TURN_BANKS)]
        for n in (0, 1):
            quantize(dz_feat[n], turned[n], E5M2)
        dz_woven = [weave_dz(0, fp) for fp in range(2)]
        quantize(dz_feat[2], turned[2], E5M2)

        for fp in range(2):
            woven = woven_tile()
            for pair in range(2):
                fetch_w(nc.scalar.copy, woven, pair, turn_w(1, fp, pair))
            square(4 + fp)
            quantize(dz_tok[0, fp], dz_woven[fp], E5M2)
            quantize(w_q[1, fp], woven, E4M3)
            neg_dz(4 + fp)
        quantize(dz_feat[3], fetch_dz(turn_dz(3)), E5M2)

        for n in (6, 7):
            square(n)
            neg_dz(n)

        accs = [sums_0(n) for n in (0, 1)]
        banks, input_woven = [], []
        for n in (0, 1):
            banks.append(turn_dz(4 + n))
            finish_0(n, accs[n])
            input_woven.append(weave(input_sb[n], 0))
        for n in (0, 1):
            quantize(dz_feat[4 + n], fetch_dz(banks[n]), E5M2)
        dz_woven = []
        for n in (0, 1):
            pending = sums_0(2 + n)
            bank = turn_dz(6 + n)
            finish_0(2 + n, pending)
            last_turned = fetch_dz(bank)
            dz_woven.append(weave_dz(1, n))
            quantize(dz_feat[6 + n], last_turned, E5M2)
            quantize(inv_q[0, n], input_woven[n], E4M3)
        for fp in range(2):
            quantize(dz_tok[1, fp], dz_woven[fp], E5M2)

        for chunk in (1, 2):
            hidden_woven = [weave(hidden_sb[tp], (chunk - 1) * PASS) for tp in range(2)]
            for tp in range(2):
                quantize(inv_q[chunk, tp], hidden_woven[tp], E4M3)

        for n in range(4, 8):
            finish_0(n, sums_0(n))
        last = K // P - 1
        for m in range(last + 1):
            result = result_tile()
            rows = slice(m * P, (m + 1) * P)
            for fp in range(2):
                columns = slice(fp * PASS, (fp + 1) * PASS)
                negate(
                    result[:, columns].rearrange("p (w u e) -> p w u e", u=2, e=2),
                    sum_1(m, fp)[:].rearrange("p (u w e) -> p w u e", u=2, e=2),
                    fp == 1 and m >= SHARED_FROM,
                )
                if m == last:
                    nc.sync.dma_start(out=out_1[rows, columns], in_=result[:, columns])
            if m < last:
                nc.sync.dma_start(out=out_1[rows, :], in_=result[:])
